import numpy as np
import ml_dtypes

BF16 = ml_dtypes.bfloat16


def bf(x):
    return np.asarray(x, np.float32).astype(BF16)


def f32(x):
    return np.asarray(x, np.float32)


def f64(x):
    return np.asarray(x).astype(np.float64)


def striped(idx):
    return np.tile(idx.reshape(-1, 16).T, (8, 1))


C, S, N, O = 256, 2048, 512, 128


def setup_inputs():
    return {"x": f32(np.random.standard_normal((C, S))), "x_dst": f32(np.random.standard_normal((C, N))), "w4a": bf(np.random.standard_normal((C, C)) / np.sqrt(C)), "b4a": f32(0.1 * np.random.standard_normal((C, 1))), "w4b": bf(np.random.standard_normal((C, O)) / np.sqrt(C)), "b4b": f32(0.1 * np.random.standard_normal((O, 1))), "offs": striped(np.random.permutation(np.tile(np.arange(S), 2))[:N])}


def reference(x, x_dst, w4a, b4a, w4b, b4b, offs):
    idx = offs[:16].T.reshape(-1)
    p = f64(x)[:, idx] * f64(x_dst)
    h = np.maximum(f64(w4a).T @ p + f64(b4a), 0.0)
    return np.maximum(f64(w4b).T @ h + f64(b4b), 0.0)

@@ -1,0 +1,69 @@
+import concourse.mybir as mybir
+
+FP32 = mybir.dt.float32
+BF16 = mybir.dt.bfloat16
+U16 = mybir.dt.uint16
+MULT = mybir.AluOpType.mult
+ADD = mybir.AluOpType.add
+MAX = mybir.AluOpType.max
+RELU = mybir.ActivationFunctionType.Relu
+
+P = 128
+C, S, N, O = 256, 2048, 512, 128
+BLOCKS = C // P
+
+FLOPS = 2 * N * (C * C + C * O)
+
+
+def tile_edgeattrs_kernel(tc, x, x_dst, w4a, b4a, w4b, b4b, offs, out):
+    nc = tc.nc
+    with (
+        tc.tile_pool(name="held", bufs=1) as held,
+        tc.psum_pool(name="psum", bufs=1) as psum,
+    ):
+        offsets = held.tile([P, N // 16], U16, name="offsets")
+        nc.sync.dma_start(offsets[:], offs)
+
+        nodes = [held.tile([P, S], FP32, name=f"nodes{c}") for c in range(BLOCKS)]
+        dst = [held.tile([P, N], FP32, name=f"dst{c}") for c in range(BLOCKS)]
+        w4a_sb = [held.tile([P, C], BF16, name=f"w4a_sb{c}") for c in range(BLOCKS)]
+        w4b_sb = [held.tile([P, O], BF16, name=f"w4b_sb{d}") for d in range(BLOCKS)]
+        b4a_sb = [held.tile([P, 1], FP32, name=f"b4a_sb{d}") for d in range(BLOCKS)]
+        b4b_sb = held.tile([P, 1], FP32, name="b4b_sb")
+        for c in range(BLOCKS):
+            rows = slice(c * P, (c + 1) * P)
+            nc.sync.dma_start(nodes[c][:], x[rows, :])
+            nc.scalar.dma_start(dst[c][:], x_dst[rows, :])
+            nc.scalar.dma_start(w4a_sb[c][:], w4a[rows, :])
+            nc.scalar.dma_start(w4b_sb[c][:], w4b[rows, :])
+            nc.gpsimd.dma_start(b4a_sb[c][:], b4a[rows, :])
+        nc.gpsimd.dma_start(b4b_sb[:], b4b)
+
+        p_bf = [held.tile([P, N], BF16, name=f"p_bf{c}") for c in range(BLOCKS)]
+        for c in range(BLOCKS):
+            p_f32 = held.tile([P, N], FP32, name=f"p_f32_{c}")
+            nc.vector.tensor_tensor(p_f32[:], nodes[c][:].indirect(offsets[:]), dst[c][:], MULT)
+            nc.scalar.copy(p_bf[c][:], p_f32[:])
+
+        h_ps = [psum.tile([P, N], FP32, name=f"h_ps{d}") for d in range(BLOCKS)]
+        h_bf = [held.tile([P, N], BF16, name=f"h_bf{d}") for d in range(BLOCKS)]
+        for d in range(BLOCKS):
+            for c in range(BLOCKS):
+                nc.tensor.matmul(
+                    h_ps[d][:],
+                    w4a_sb[c][:, d * P : (d + 1) * P],
+                    p_bf[c][:],
+                    start=(c == 0),
+                    stop=(c == BLOCKS - 1),
+                )
+        nc.scalar.activation(h_bf[0][:], h_ps[0][:], RELU, bias=b4a_sb[0][:])
+        nc.vector.tensor_scalar(h_bf[1][:], h_ps[1][:], b4a_sb[1][:], 0.0, ADD, MAX)
+
+        out_ps = psum.tile([P, N], FP32, name="out_ps")
+        for d in range(BLOCKS):
+            nc.tensor.matmul(
+                out_ps[:], w4b_sb[d][:], h_bf[d][:], start=(d == 0), stop=(d == BLOCKS - 1)
+            )
+        out_sb = held.tile([P, N], FP32, name="out_sb")
+        nc.scalar.activation(out_sb[:], out_ps[:], RELU, bias=b4b_sb[:])
+        nc.sync.dma_start(out, out_sb[:])

@@ -11,6 +11,8 @@ RELU = mybir.ActivationFunctionType.Relu
 P = 128
 C, S, N, O = 256, 2048, 512, 128
 BLOCKS = C // P
+PIECE = 128
+PIECES = N // PIECE
 
 FLOPS = 2 * N * (C * C + C * O)
 
@@ -19,7 +21,8 @@ def tile_edgeattrs_kernel(tc, x, x_dst, w4a, b4a, w4b, b4b, offs, out):
     nc = tc.nc
     with (
         tc.tile_pool(name="held", bufs=1) as held,
-        tc.psum_pool(name="psum", bufs=1) as psum,
+        tc.tile_pool(name="ring", bufs=PIECES) as ring,
+        tc.psum_pool(name="psum", bufs=2) as psum,
     ):
         offsets = held.tile([P, N // 16], U16, name="offsets")
         nc.sync.dma_start(offsets[:], offs)
@@ -40,30 +43,40 @@ def tile_edgeattrs_kernel(tc, x, x_dst, w4a, b4a, w4b, b4b, offs, out):
         nc.gpsimd.dma_start(b4b_sb[:], b4b)
 
         p_bf = [held.tile([P, N], BF16, name=f"p_bf{c}") for c in range(BLOCKS)]
-        for c in range(BLOCKS):
-            p_f32 = held.tile([P, N], FP32, name=f"p_f32_{c}")
-            nc.vector.tensor_tensor(p_f32[:], nodes[c][:].indirect(offsets[:]), dst[c][:], MULT)
-            nc.scalar.copy(p_bf[c][:], p_f32[:])
-
-        h_ps = [psum.tile([P, N], FP32, name=f"h_ps{d}") for d in range(BLOCKS)]
         h_bf = [held.tile([P, N], BF16, name=f"h_bf{d}") for d in range(BLOCKS)]
-        for d in range(BLOCKS):
-            for c in range(BLOCKS):
-                nc.tensor.matmul(
-                    h_ps[d][:],
-                    w4a_sb[c][:, d * P : (d + 1) * P],
-                    p_bf[c][:],
-                    start=(c == 0),
-                    stop=(c == BLOCKS - 1),
-                )
-        nc.scalar.activation(h_bf[0][:], h_ps[0][:], RELU, bias=b4a_sb[0][:])
-        nc.vector.tensor_scalar(h_bf[1][:], h_ps[1][:], b4a_sb[1][:], 0.0, ADD, MAX)
-
-        out_ps = psum.tile([P, N], FP32, name="out_ps")
-        for d in range(BLOCKS):
-            nc.tensor.matmul(
-                out_ps[:], w4b_sb[d][:], h_bf[d][:], start=(d == 0), stop=(d == BLOCKS - 1)
-            )
         out_sb = held.tile([P, N], FP32, name="out_sb")
-        nc.scalar.activation(out_sb[:], out_ps[:], RELU, bias=b4b_sb[:])
-        nc.sync.dma_start(out, out_sb[:])
+
+        def product(c, j):
+            edges = slice(j * PIECE, (j + 1) * PIECE)
+            listed = offsets[:, j * (PIECE // 16) : (j + 1) * (PIECE // 16)]
+            p_f32 = ring.tile([P, PIECE], FP32, name="p_f32")
+            nc.vector.tensor_tensor(p_f32[:], nodes[c][:].indirect(listed), dst[c][:, edges], MULT)
+            nc.scalar.copy(p_bf[c][:, edges], p_f32[:])
+
+        for j in range(PIECES):
+            product(0, j)
+
+        for j in range(PIECES):
+            edges = slice(j * PIECE, (j + 1) * PIECE)
+            product(1, j)
+
+            h_ps = [psum.tile([P, PIECE], FP32, name=f"h_ps{d}") for d in range(BLOCKS)]
+            for d in range(BLOCKS):
+                for c in range(BLOCKS):
+                    nc.tensor.matmul(
+                        h_ps[d][:],
+                        w4a_sb[c][:, d * P : (d + 1) * P],
+                        p_bf[c][:, edges],
+                        start=(c == 0),
+                        stop=(c == BLOCKS - 1),
+                    )
+            nc.scalar.activation(h_bf[0][:, edges], h_ps[0][:], RELU, bias=b4a_sb[0][:])
+            nc.vector.tensor_scalar(h_bf[1][:, edges], h_ps[1][:], b4a_sb[1][:], 0.0, ADD, MAX)
+
+            out_ps = psum.tile([P, PIECE], FP32, name="out_ps")
+            for d in range(BLOCKS):
+                nc.tensor.matmul(
+                    out_ps[:], w4b_sb[d][:], h_bf[d][:, edges], start=(d == 0), stop=(d == BLOCKS - 1)
+                )
+            nc.scalar.activation(out_sb[:, edges], out_ps[:], RELU, bias=b4b_sb[:])
+            nc.sync.dma_start(out[:, edges], out_sb[:, edges])

@@ -13,6 +13,7 @@ C, S, N, O = 256, 2048, 512, 128
 BLOCKS = C // P
 PIECE = 128
 PIECES = N // PIECE
+BANKS = 8
 
 FLOPS = 2 * N * (C * C + C * O)
 
@@ -22,7 +23,7 @@ def tile_edgeattrs_kernel(tc, x, x_dst, w4a, b4a, w4b, b4b, offs, out):
     with (
         tc.tile_pool(name="held", bufs=1) as held,
         tc.tile_pool(name="ring", bufs=PIECES) as ring,
-        tc.psum_pool(name="psum", bufs=2) as psum,
+        tc.psum_pool(name="psum", bufs=BANKS) as psum,
     ):
         offsets = held.tile([P, N // 16], U16, name="offsets")
         nc.sync.dma_start(offsets[:], offs)
@@ -33,50 +34,53 @@ def tile_edgeattrs_kernel(tc, x, x_dst, w4a, b4a, w4b, b4b, offs, out):
         w4b_sb = [held.tile([P, O], BF16, name=f"w4b_sb{d}") for d in range(BLOCKS)]
         b4a_sb = [held.tile([P, 1], FP32, name=f"b4a_sb{d}") for d in range(BLOCKS)]
         b4b_sb = held.tile([P, 1], FP32, name="b4b_sb")
+        for d in range(BLOCKS):
+            nc.scalar.dma_start(b4a_sb[d][:], b4a[d * P : (d + 1) * P, :])
+        nc.scalar.dma_start(b4b_sb[:], b4b)
         for c in range(BLOCKS):
             rows = slice(c * P, (c + 1) * P)
             nc.sync.dma_start(nodes[c][:], x[rows, :])
             nc.scalar.dma_start(dst[c][:], x_dst[rows, :])
             nc.scalar.dma_start(w4a_sb[c][:], w4a[rows, :])
             nc.scalar.dma_start(w4b_sb[c][:], w4b[rows, :])
-            nc.gpsimd.dma_start(b4a_sb[c][:], b4a[rows, :])
-        nc.gpsimd.dma_start(b4b_sb[:], b4b)
 
         p_bf = [held.tile([P, N], BF16, name=f"p_bf{c}") for c in range(BLOCKS)]
         h_bf = [held.tile([P, N], BF16, name=f"h_bf{d}") for d in range(BLOCKS)]
         out_sb = held.tile([P, N], FP32, name="out_sb")
+        h_ps = [
+            [psum.tile([P, PIECE], FP32, name=f"h_ps{j}_{d}", tag="bank") for d in range(BLOCKS)]
+            for j in range(PIECES)
+        ]
 
-        def product(c, j):
+        def half_of_layer_1(c, j):
             edges = slice(j * PIECE, (j + 1) * PIECE)
             listed = offsets[:, j * (PIECE // 16) : (j + 1) * (PIECE // 16)]
             p_f32 = ring.tile([P, PIECE], FP32, name="p_f32")
             nc.vector.tensor_tensor(p_f32[:], nodes[c][:].indirect(listed), dst[c][:, edges], MULT)
             nc.scalar.copy(p_bf[c][:, edges], p_f32[:])
+            for d in range(BLOCKS):
+                nc.tensor.matmul(
+                    h_ps[j][d][:],
+                    w4a_sb[c][:, d * P : (d + 1) * P],
+                    p_bf[c][:, edges],
+                    start=(c == 0),
+                    stop=(c == BLOCKS - 1),
+                )
 
         for j in range(PIECES):
-            product(0, j)
+            half_of_layer_1(0, j)
 
         for j in range(PIECES):
             edges = slice(j * PIECE, (j + 1) * PIECE)
-            product(1, j)
+            half_of_layer_1(1, j)
 
-            h_ps = [psum.tile([P, PIECE], FP32, name=f"h_ps{d}") for d in range(BLOCKS)]
-            for d in range(BLOCKS):
-                for c in range(BLOCKS):
-                    nc.tensor.matmul(
-                        h_ps[d][:],
-                        w4a_sb[c][:, d * P : (d + 1) * P],
-                        p_bf[c][:, edges],
-                        start=(c == 0),
-                        stop=(c == BLOCKS - 1),
-                    )
-            nc.scalar.activation(h_bf[0][:, edges], h_ps[0][:], RELU, bias=b4a_sb[0][:])
-            nc.vector.tensor_scalar(h_bf[1][:, edges], h_ps[1][:], b4a_sb[1][:], 0.0, ADD, MAX)
+            nc.scalar.activation(h_bf[0][:, edges], h_ps[j][0][:], RELU, bias=b4a_sb[0][:])
+            nc.vector.tensor_scalar(h_bf[1][:, edges], h_ps[j][1][:], b4a_sb[1][:], 0.0, ADD, MAX)
 
-            out_ps = psum.tile([P, PIECE], FP32, name="out_ps")
+            out_ps = psum.tile([P, PIECE], FP32, name="out_ps", tag="bank")
             for d in range(BLOCKS):
                 nc.tensor.matmul(
                     out_ps[:], w4b_sb[d][:], h_bf[d][:, edges], start=(d == 0), stop=(d == BLOCKS - 1)
                 )
-            nc.scalar.activation(out_sb[:, edges], out_ps[:], RELU, bias=b4b_sb[:])
+            nc.vector.tensor_scalar(out_sb[:, edges], out_ps[:], b4b_sb[:], 0.0, ADD, MAX)
             nc.sync.dma_start(out[:, edges], out_sb[:, edges])

@@ -11,7 +11,7 @@ RELU = mybir.ActivationFunctionType.Relu
 P = 128
 C, S, N, O = 256, 2048, 512, 128
 BLOCKS = C // P
-PIECE = 128
+PIECE = 256
 PIECES = N // PIECE
 BANKS = 8
 

@@ -11,7 +11,7 @@ RELU = mybir.ActivationFunctionType.Relu
 P = 128
 C, S, N, O = 256, 2048, 512, 128
 BLOCKS = C // P
-PIECE = 256
+PIECE = 128
 PIECES = N // PIECE
 BANKS = 8
 
@@ -34,15 +34,17 @@ def tile_edgeattrs_kernel(tc, x, x_dst, w4a, b4a, w4b, b4b, offs, out):
         w4b_sb = [held.tile([P, O], BF16, name=f"w4b_sb{d}") for d in range(BLOCKS)]
         b4a_sb = [held.tile([P, 1], FP32, name=f"b4a_sb{d}") for d in range(BLOCKS)]
         b4b_sb = held.tile([P, 1], FP32, name="b4b_sb")
+        block = [slice(c * P, (c + 1) * P) for c in range(BLOCKS)]
+        nc.sync.dma_start(nodes[0][:], x[block[0], :])
+        nc.sync.dma_start(nodes[1][:], x[block[1], :])
+        nc.scalar.dma_start(dst[0][:], x_dst[block[0], :])
+        nc.scalar.dma_start(w4a_sb[0][:], w4a[block[0], :])
+        nc.scalar.dma_start(dst[1][:], x_dst[block[1], :])
+        nc.sync.dma_start(w4a_sb[1][:], w4a[block[1], :])
         for d in range(BLOCKS):
-            nc.scalar.dma_start(b4a_sb[d][:], b4a[d * P : (d + 1) * P, :])
+            nc.scalar.dma_start(b4a_sb[d][:], b4a[block[d], :])
+            nc.sync.dma_start(w4b_sb[d][:], w4b[block[d], :])
         nc.scalar.dma_start(b4b_sb[:], b4b)
-        for c in range(BLOCKS):
-            rows = slice(c * P, (c + 1) * P)
-            nc.sync.dma_start(nodes[c][:], x[rows, :])
-            nc.scalar.dma_start(dst[c][:], x_dst[rows, :])
-            nc.scalar.dma_start(w4a_sb[c][:], w4a[rows, :])
-            nc.scalar.dma_start(w4b_sb[c][:], w4b[rows, :])
 
         p_bf = [held.tile([P, N], BF16, name=f"p_bf{c}") for c in range(BLOCKS)]
         h_bf = [held.tile([P, N], BF16, name=f"h_bf{d}") for d in range(BLOCKS)]

@@ -11,9 +11,11 @@ RELU = mybir.ActivationFunctionType.Relu
 P = 128
 C, S, N, O = 256, 2048, 512, 128
 BLOCKS = C // P
-PIECE = 128
-PIECES = N // PIECE
+WIDTHS = (192, 160, 96, 64)
+PIECES = len(WIDTHS)
+STARTS = [sum(WIDTHS[:j]) for j in range(PIECES)]
 BANKS = 8
+STORE = 128
 
 FLOPS = 2 * N * (C * C + C * O)
 
@@ -50,14 +52,14 @@ def tile_edgeattrs_kernel(tc, x, x_dst, w4a, b4a, w4b, b4b, offs, out):
         h_bf = [held.tile([P, N], BF16, name=f"h_bf{d}") for d in range(BLOCKS)]
         out_sb = held.tile([P, N], FP32, name="out_sb")
         h_ps = [
-            [psum.tile([P, PIECE], FP32, name=f"h_ps{j}_{d}", tag="bank") for d in range(BLOCKS)]
+            [psum.tile([P, WIDTHS[j]], FP32, name=f"h_ps{j}_{d}", tag="bank") for d in range(BLOCKS)]
             for j in range(PIECES)
         ]
 
         def half_of_layer_1(c, j):
-            edges = slice(j * PIECE, (j + 1) * PIECE)
-            listed = offsets[:, j * (PIECE // 16) : (j + 1) * (PIECE // 16)]
-            p_f32 = ring.tile([P, PIECE], FP32, name="p_f32")
+            edges = slice(STARTS[j], STARTS[j] + WIDTHS[j])
+            listed = offsets[:, edges.start // 16 : edges.stop // 16]
+            p_f32 = ring.tile([P, WIDTHS[j]], FP32, name="p_f32")
             nc.vector.tensor_tensor(p_f32[:], nodes[c][:].indirect(listed), dst[c][:, edges], MULT)
             nc.scalar.copy(p_bf[c][:, edges], p_f32[:])
             for d in range(BLOCKS):
@@ -72,17 +74,20 @@ def tile_edgeattrs_kernel(tc, x, x_dst, w4a, b4a, w4b, b4b, offs, out):
         for j in range(PIECES):
             half_of_layer_1(0, j)
 
+        stored = 0
         for j in range(PIECES):
-            edges = slice(j * PIECE, (j + 1) * PIECE)
+            edges = slice(STARTS[j], STARTS[j] + WIDTHS[j])
             half_of_layer_1(1, j)
 
             nc.scalar.activation(h_bf[0][:, edges], h_ps[j][0][:], RELU, bias=b4a_sb[0][:])
             nc.vector.tensor_scalar(h_bf[1][:, edges], h_ps[j][1][:], b4a_sb[1][:], 0.0, ADD, MAX)
 
-            out_ps = psum.tile([P, PIECE], FP32, name="out_ps", tag="bank")
+            out_ps = psum.tile([P, WIDTHS[j]], FP32, name="out_ps", tag="bank")
             for d in range(BLOCKS):
                 nc.tensor.matmul(
                     out_ps[:], w4b_sb[d][:], h_bf[d][:, edges], start=(d == 0), stop=(d == BLOCKS - 1)
                 )
             nc.vector.tensor_scalar(out_sb[:, edges], out_ps[:], b4b_sb[:], 0.0, ADD, MAX)
-            nc.sync.dma_start(out[:, edges], out_sb[:, edges])
+            while stored + STORE <= edges.stop:
+                nc.sync.dma_start(out[:, stored : stored + STORE], out_sb[:, stored : stored + STORE])
+                stored += STORE

@@ -34,9 +34,10 @@ def tile_edgeattrs_kernel(tc, x, x_dst, w4a, b4a, w4b, b4b, offs, out):
         dst = [held.tile([P, N], FP32, name=f"dst{c}") for c in range(BLOCKS)]
         w4a_sb = [held.tile([P, C], BF16, name=f"w4a_sb{c}") for c in range(BLOCKS)]
         w4b_sb = [held.tile([P, O], BF16, name=f"w4b_sb{d}") for d in range(BLOCKS)]
-        b4a_sb = [held.tile([P, 1], FP32, name=f"b4a_sb{d}") for d in range(BLOCKS)]
-        b4b_sb = held.tile([P, 1], FP32, name="b4b_sb")
+        bias_rows = held.tile([1, C + O], FP32, name="bias_rows")
         block = [slice(c * P, (c + 1) * P) for c in range(BLOCKS)]
+        nc.sync.dma_start(bias_rows[:, 0:C], b4a.rearrange("c o -> o c"))
+        nc.sync.dma_start(bias_rows[:, C : C + O], b4b.rearrange("m o -> o m"))
         nc.sync.dma_start(nodes[0][:], x[block[0], :])
         nc.sync.dma_start(nodes[1][:], x[block[1], :])
         nc.scalar.dma_start(dst[0][:], x_dst[block[0], :])
@@ -44,9 +45,20 @@ def tile_edgeattrs_kernel(tc, x, x_dst, w4a, b4a, w4b, b4b, offs, out):
         nc.scalar.dma_start(dst[1][:], x_dst[block[1], :])
         nc.sync.dma_start(w4a_sb[1][:], w4a[block[1], :])
         for d in range(BLOCKS):
-            nc.scalar.dma_start(b4a_sb[d][:], b4a[block[d], :])
             nc.sync.dma_start(w4b_sb[d][:], w4b[block[d], :])
-        nc.scalar.dma_start(b4b_sb[:], b4b)
+
+        one = held.tile([1, 1], FP32, name="one")
+        nc.vector.memset(one[:], 1.0)
+        RUNS = (C + O) // P
+        bias_ps = psum.tile([P, RUNS], FP32, name="bias_ps", tag="bank")
+        for r in range(RUNS):
+            nc.tensor.matmul(
+                bias_ps[:, r : r + 1], bias_rows[:, r * P : (r + 1) * P], one[:], start=True, stop=True
+            )
+        bias_sb = held.tile([P, RUNS], FP32, name="bias_sb")
+        nc.vector.tensor_copy(bias_sb[:], bias_ps[:])
+        b4a_sb = [bias_sb[:, d : d + 1] for d in range(BLOCKS)]
+        b4b_sb = bias_sb[:, BLOCKS : BLOCKS + 1]
 
         p_bf = [held.tile([P, N], BF16, name=f"p_bf{c}") for c in range(BLOCKS)]
         h_bf = [held.tile([P, N], BF16, name=f"h_bf{d}") for d in range(BLOCKS)]
@@ -79,15 +91,15 @@ def tile_edgeattrs_kernel(tc, x, x_dst, w4a, b4a, w4b, b4b, offs, out):
             edges = slice(STARTS[j], STARTS[j] + WIDTHS[j])
             half_of_layer_1(1, j)
 
-            nc.scalar.activation(h_bf[0][:, edges], h_ps[j][0][:], RELU, bias=b4a_sb[0][:])
-            nc.vector.tensor_scalar(h_bf[1][:, edges], h_ps[j][1][:], b4a_sb[1][:], 0.0, ADD, MAX)
+            nc.scalar.activation(h_bf[0][:, edges], h_ps[j][0][:], RELU, bias=b4a_sb[0])
+            nc.vector.tensor_scalar(h_bf[1][:, edges], h_ps[j][1][:], b4a_sb[1], 0.0, ADD, MAX)
 
             out_ps = psum.tile([P, WIDTHS[j]], FP32, name="out_ps", tag="bank")
             for d in range(BLOCKS):
                 nc.tensor.matmul(
                     out_ps[:], w4b_sb[d][:], h_bf[d][:, edges], start=(d == 0), stop=(d == BLOCKS - 1)
                 )
-            nc.vector.tensor_scalar(out_sb[:, edges], out_ps[:], b4b_sb[:], 0.0, ADD, MAX)
+            nc.vector.tensor_scalar(out_sb[:, edges], out_ps[:], b4b_sb, 0.0, ADD, MAX)
             while stored + STORE <= edges.stop:
                 nc.sync.dma_start(out[:, stored : stored + STORE], out_sb[:, stored : stored + STORE])
                 stored += STORE

import concourse.mybir as mybir

FP32 = mybir.dt.float32
BF16 = mybir.dt.bfloat16
U16 = mybir.dt.uint16
MULT = mybir.AluOpType.mult
ADD = mybir.AluOpType.add
MAX = mybir.AluOpType.max
RELU = mybir.ActivationFunctionType.Relu

P = 128
C, S, N, O = 256, 2048, 512, 128
BLOCKS = C // P
WIDTHS = (192, 160, 96, 64)
PIECES = len(WIDTHS)
STARTS = [sum(WIDTHS[:j]) for j in range(PIECES)]
BANKS = 8
STORE = 128

FLOPS = 2 * N * (C * C + C * O)


def tile_edgeattrs_kernel(tc, x, x_dst, w4a, b4a, w4b, b4b, offs, out):
    nc = tc.nc
    with (
        tc.tile_pool(name="held", bufs=1) as held,
        tc.tile_pool(name="ring", bufs=PIECES) as ring,
        tc.psum_pool(name="psum", bufs=BANKS) as psum,
    ):
        offsets = held.tile([P, N // 16], U16, name="offsets")
        nc.sync.dma_start(offsets[:], offs)

        nodes = [held.tile([P, S], FP32, name=f"nodes{c}") for c in range(BLOCKS)]
        dst = [held.tile([P, N], FP32, name=f"dst{c}") for c in range(BLOCKS)]
        w4a_sb = [held.tile([P, C], BF16, name=f"w4a_sb{c}") for c in range(BLOCKS)]
        w4b_sb = [held.tile([P, O], BF16, name=f"w4b_sb{d}") for d in range(BLOCKS)]
        bias_rows = held.tile([1, C + O], FP32, name="bias_rows")
        block = [slice(c * P, (c + 1) * P) for c in range(BLOCKS)]
        nc.sync.dma_start(bias_rows[:, 0:C], b4a.rearrange("c o -> o c"))
        nc.sync.dma_start(bias_rows[:, C : C + O], b4b.rearrange("m o -> o m"))
        nc.sync.dma_start(nodes[0][:], x[block[0], :])
        nc.sync.dma_start(nodes[1][:], x[block[1], :])
        nc.scalar.dma_start(dst[0][:], x_dst[block[0], :])
        nc.scalar.dma_start(w4a_sb[0][:], w4a[block[0], :])
        nc.scalar.dma_start(dst[1][:], x_dst[block[1], :])
        nc.sync.dma_start(w4a_sb[1][:], w4a[block[1], :])
        for d in range(BLOCKS):
            nc.sync.dma_start(w4b_sb[d][:], w4b[block[d], :])

        one = held.tile([1, 1], FP32, name="one")
        nc.vector.memset(one[:], 1.0)
        RUNS = (C + O) // P
        bias_ps = psum.tile([P, RUNS], FP32, name="bias_ps", tag="bank")
        for r in range(RUNS):
            nc.tensor.matmul(
                bias_ps[:, r : r + 1], bias_rows[:, r * P : (r + 1) * P], one[:], start=True, stop=True
            )
        bias_sb = held.tile([P, RUNS], FP32, name="bias_sb")
        nc.vector.tensor_copy(bias_sb[:], bias_ps[:])
        b4a_sb = [bias_sb[:, d : d + 1] for d in range(BLOCKS)]
        b4b_sb = bias_sb[:, BLOCKS : BLOCKS + 1]

        p_bf = [held.tile([P, N], BF16, name=f"p_bf{c}") for c in range(BLOCKS)]
        h_bf = [held.tile([P, N], BF16, name=f"h_bf{d}") for d in range(BLOCKS)]
        out_sb = held.tile([P, N], FP32, name="out_sb")
        h_ps = [
            [psum.tile([P, WIDTHS[j]], FP32, name=f"h_ps{j}_{d}", tag="bank") for d in range(BLOCKS)]
            for j in range(PIECES)
        ]

        def half_of_layer_1(c, j):
            edges = slice(STARTS[j], STARTS[j] + WIDTHS[j])
            listed = offsets[:, edges.start // 16 : edges.stop // 16]
            p_f32 = ring.tile([P, WIDTHS[j]], FP32, name="p_f32")
            nc.vector.tensor_tensor(p_f32[:], nodes[c][:].indirect(listed), dst[c][:, edges], MULT)
            nc.scalar.copy(p_bf[c][:, edges], p_f32[:])
            for d in range(BLOCKS):
                nc.tensor.matmul(
                    h_ps[j][d][:],
                    w4a_sb[c][:, d * P : (d + 1) * P],
                    p_bf[c][:, edges],
                    start=(c == 0),
                    stop=(c == BLOCKS - 1),
                )

        for j in range(PIECES):
            half_of_layer_1(0, j)

        stored = 0
        for j in range(PIECES):
            edges = slice(STARTS[j], STARTS[j] + WIDTHS[j])
            half_of_layer_1(1, j)

            nc.scalar.activation(h_bf[0][:, edges], h_ps[j][0][:], RELU, bias=b4a_sb[0])
            nc.vector.tensor_scalar(h_bf[1][:, edges], h_ps[j][1][:], b4a_sb[1], 0.0, ADD, MAX)

            out_ps = psum.tile([P, WIDTHS[j]], FP32, name="out_ps", tag="bank")
            for d in range(BLOCKS):
                nc.tensor.matmul(
                    out_ps[:], w4b_sb[d][:], h_bf[d][:, edges], start=(d == 0), stop=(d == BLOCKS - 1)
                )
            nc.vector.tensor_scalar(out_sb[:, edges], out_ps[:], b4b_sb, 0.0, ADD, MAX)
            while stored + STORE <= edges.stop:
                nc.sync.dma_start(out[:, stored : stored + STORE], out_sb[:, stored : stored + STORE])
                stored += STORE
